import numpy as np
import ml_dtypes


def mxq(x, axis, fmt="e4m3"):
    dtype, down = {"e4m3": (ml_dtypes.float8_e4m3fn, 7), "e5m2": (ml_dtypes.float8_e5m2, 14)}[fmt]
    v = np.moveaxis(np.asarray(x, np.float32).astype(ml_dtypes.bfloat16).astype(np.float64), axis, -1)
    blocks = v.reshape(v.shape[:-1] + (-1, 32))
    amax = np.abs(blocks).max(-1, keepdims=True)
    byte = np.maximum(np.where(amax > 0, np.frexp(amax)[1] - 1 + 127, 0) - down, 1)
    scale = np.exp2(byte - 127.0)
    codes = (blocks / scale).astype(np.float32).astype(dtype).astype(np.float64)
    return np.moveaxis((codes * scale).reshape(v.shape), -1, axis)


WIDE = False


def mx_kscale(k):
    if not WIDE:
        return np.ones(k)
    levels = np.array([10, -10, 5, -5, 0])
    if k % 512:
        return np.exp2(np.random.permutation(np.resize(levels, k // 32))).repeat(32)
    a = np.empty((k // 512, 16))
    for p in range(k // 512):
        a[p, :8] = np.random.permutation(np.resize(levels, 8))
        for g in range(8):
            far = levels[np.abs(levels - a[p, g]) >= 10]
            a[p, g + 8] = far[np.random.randint(len(far))]
    return np.exp2(a.ravel()).repeat(32)


BF16 = ml_dtypes.bfloat16


def bf(x):
    return np.asarray(x, np.float32).astype(BF16)


def f64(x):
    return np.asarray(x).astype(np.float64)


B, D0, D1, D2, D3 = 512, 2048, 2048, 2048, 2048
HEBB = 0.01
RATE = 0.001
BATCH_NUM = 1
C = HEBB * RATE / BATCH_NUM


def centred(s):
    return s / np.exp2(np.round(np.log2(s.mean())))


def draw0():
    s, t = centred(mx_kscale(D0)), centred(mx_kscale(D1))
    return {"x": bf((4.0 + 3.0 * np.random.standard_normal((B, D0))) * s),
            "W1": bf(np.random.standard_normal((D1, D0)) * 0.9 / np.sqrt(D0) / s[None, :] * t[:, None]),
            "b1": bf((3.0 + 1.5 * np.random.standard_normal(D1)) * t),
            "W2": bf(np.random.standard_normal((D2, D1)) * 0.9 / np.sqrt(D1) / t[None, :]),
            "b2": bf(3.0 + 1.5 * np.random.standard_normal(D2))}


def core(x, W1, b1, W2, b2):
    x = f64(x)
    v1 = np.maximum((mxq(x, 1, "e4m3") @ mxq(f64(W1), 1, "e4m3").T) + f64(b1), 0.0)
    m1 = np.mean(v1, axis=0)
    h = v1 + np.sum(x, axis=1, keepdims=True) * (C * m1)[None, :]
    v2 = np.maximum((mxq(h, 1, "e4m3") @ mxq(f64(W2), 1, "e4m3").T) + f64(b2), 0.0)
    m2 = np.mean(v2, axis=0)
    out = v2 + np.sum(h, axis=1, keepdims=True) * (C * m2)[None, :]
    return out, m1, m2


def e4m3fn_bytes(y):
    return np.clip(np.asarray(y, np.float64), -448.0, 448.0).astype(np.float32).astype(ml_dtypes.float8_e4m3fn).view(np.uint8)


def e4m3fn_values(b):
    return np.asarray(b, np.uint8).view(ml_dtypes.float8_e4m3fn).astype(np.float64)


def setup_inputs():
    d = draw0()
    x0 = np.asarray(d['W2']).astype(np.float64)
    s = (np.max(np.abs(x0), axis=(0,), keepdims=True) / 448.0).astype(np.float32)
    out = {}
    for k, v in d.items():
        if k == 'W2':
            out['W2_bytes'] = e4m3fn_bytes(x0 / s.astype(np.float64))
            out['W2_scale'] = s
        else:
            out[k] = v
    return out


def reference(x, W1, b1, W2_bytes, W2_scale, b2):
    return core(x, W1, b1, e4m3fn_values(W2_bytes) * W2_scale.astype(np.float64), b2)

from contextlib import ExitStack

import concourse.mybir as mybir
from concourse.masks import make_identity

B, D = 512, 2048
COEF = 0.01 * 0.001 / 1
FLOPS = 2 * 2 * B * D * D

F32 = mybir.dt.float32
BF16 = mybir.dt.bfloat16
U32 = mybir.dt.uint32
U8 = mybir.dt.uint8
FP8 = mybir.dt.float8_e4m3fn
FP8X4 = mybir.dt.float8_e4m3fn_x4
ACT = mybir.ActivationFunctionType
ALU = mybir.AluOpType
AX = mybir.AxisListType

P = 128
RAW_BUFS = 10
E_VECTOR = {1: (0,), 8: (3,), 12: (1,), 14: (0,), 15: (0,)}
SUMS = {0: (0, 1), 1: (2,), 2: (3,)}
NG = 4
NRT = 4
NPAIR = 8

PROD_HEAD = [0, 0, 0, 0]
PROD = [0, 2, 1, 1, 1, 1, 1, 1, 0, 2, 1, 1, 1, 1, 2, 0]


def tile_optimalnet_pa_kernel(tc, x, W1, b1, W2_bytes, W2_scale, b2, out_0, out_1, out_2):
    nc = tc.nc
    with ExitStack() as ctx:
        const = ctx.enter_context(tc.tile_pool(name="const", bufs=1))
        rawp = ctx.enter_context(tc.tile_pool(name="rawp", bufs=RAW_BUFS))
        bytesp = ctx.enter_context(tc.tile_pool(name="bytesp", bufs=4))
        valp = ctx.enter_context(tc.tile_pool(name="valp", bufs=8))
        grp = ctx.enter_context(tc.tile_pool(name="grp", bufs=2))
        codep = ctx.enter_context(tc.tile_pool(name="codep", bufs=3))
        v1p = ctx.enter_context(tc.tile_pool(name="v1p", bufs=4))
        hp = ctx.enter_context(tc.tile_pool(name="hp", bufs=2))
        trp = ctx.enter_context(tc.psum_pool(name="trp", bufs=4))
        mmp = ctx.enter_context(tc.psum_pool(name="mmp", bufs=4))
        ctx.enter_context(tc.manual_schedule())

        sraw = const.tile([P, 16], F32, name="sraw")
        nc.scalar.dma_start(out=sraw[:], in_=W2_scale.rearrange("o (p j) -> p (o j)", j=16))
        b1h = const.tile([P, 4, 4], BF16, name="b1h")
        nc.scalar.dma_start(out=b1h[:], in_=b1.rearrange("(g p t) -> p g t", p=P, t=4))
        b2h = const.tile([P, NPAIR, 2], BF16, name="b2h")
        nc.scalar.dma_start(out=b2h[:], in_=b2.rearrange("(j p t) -> p j t", p=P, t=2))

        w1v = W1.rearrange("(g m t) k -> g t m k", m=P, t=4)
        w2v = W2_bytes.rearrange("(j m t) k -> j m t k", m=P, t=2)
        x_raw, w1_raw, w2_raw = [], [], []

        def load_x(rt):
            x_t = rawp.tile([P, D], BF16, name="raw", tag="raw", align_bytes=64)
            nc.sync.dma_start(out=x_t[:], in_=x[rt * P : (rt + 1) * P, :])
            x_raw.append(x_t)

        def load_w1(i):
            w_t = rawp.tile([P, D], BF16, name="raw", tag="raw", align_bytes=64)
            nc.sync.dma_start(out=w_t[:], in_=w1v[i // 4, i % 4])
            w1_raw.append(w_t)

        def load_w2(j):
            w_b = bytesp.tile([P, 2, D], U8, name="w_b", align_bytes=64)
            nc.sync.dma_start(out=w_b[:], in_=w2v[j])
            w2_raw.append(w_b)

        for rt in range(NRT):
            load_x(rt)
        for i in range(4):
            load_w1(i)
        load_w2(0)
        load_w1(4)
        load_w1(5)
        load_w2(1)

        ident = const.tile([P, P], F32, name="ident")
        make_identity(nc, ident[:])
        m1pad = const.tile([P, 4, P], F32, name="m1pad")
        nc.gpsimd.memset(m1pad[:], 0.0)
        m2pad = const.tile([P, 2, P], F32, name="m2pad")
        nc.gpsimd.memset(m2pad[:], 0.0)
        ones_f = const.tile([P, P], F32, name="ones_f")
        nc.vector.memset(ones_f[:], 1.0)
        warm = const.tile([P, 1], F32, name="warm")
        nc.scalar.activation(out=warm[:], in_=ones_f[:, 0:1], func=ACT.Relu)

        sc = const.tile([P, D], F32, name="sc", align_bytes=64)
        sc_view = sc[:].rearrange("q (p j) -> q p j", j=16)
        for b in range(4):
            bank = mmp.tile([P, 4, P], F32, name="mm")
            for j in range(4):
                col = 4 * b + j
                nc.tensor.transpose(bank[:, j, :], sraw[:, col : col + 1].to_broadcast([P, P]), ident[:])
            if b < 4:
                nc.scalar.copy(out=sc_view[:, :, 4 * b : 4 * b + 4], in_=bank[:].rearrange("q j p -> q p j"))
            else:
                nc.vector.tensor_copy(out=sc_view[:, :, 4 * b : 4 * b + 4], in_=bank[:].rearrange("q j p -> q p j"))

        w2_val = {}
        prod_next = [0]

        def products(count):
            for c in range(count):
                n = prod_next[0]
                if n >= 2 * NPAIR:
                    return
                prod_next[0] = n + 1
                val = valp.tile([P, D], BF16, name="val", align_bytes=64)
                w2_val[n] = val
                nc.vector.tensor_tensor(
                    out=val[:], in0=w2_raw[n // 2][:, n % 2, :].bitcast(FP8), in1=sc[:], op=ALU.mult
                )

        def turn(src, g0):
            words = src[:].bitcast(F32)
            bank = trp.tile([P, 2, 2, P], F32, name="tr")
            for g in range(2):
                for u in range(2):
                    w0 = 256 * (g0 + g)
                    nc.tensor.transpose(bank[:, g, u, :], words[:, w0 + u : w0 + 256 : 2], ident[:])
            return bank

        sx_col = const.tile([P, NRT], F32, name="sx_col")
        summed = [0]

        def x_sum(rt):
            junk = hp.tile([P, D], BF16, name="hg", bufs=1, align_bytes=64)
            nc.scalar.activation(out=junk[:], in_=x_raw[rt][:], func=ACT.Identity, accum_out=sx_col[:, rt : rt + 1])
            summed[0] = rt + 1

        def load_ahead(turned):
            room = RAW_BUFS + (summed[0] - NRT if summed[0] < NRT else turned)
            while len(w1_raw) < min(2 * NPAIR, room):
                load_w1(len(w1_raw))

        xg = const.tile([P, NG, NRT, P, 4], BF16, name="xg", align_bytes=64)
        for rt in range(NRT):
            for half in range(2):
                bank = turn(x_raw[rt], 2 * half)
                dst = xg[:, 2 * half : 2 * half + 2, rt, :, :].bitcast(F32)
                nc.vector.tensor_copy(out=dst, in_=bank[:].rearrange("p g u r -> p g r u"))
            if rt in SUMS[0]:
                x_sum(rt)
            products(PROD_HEAD[rt])
        load_ahead(0)

        b1f = const.tile([P, 4, 4], F32, name="b1f")
        nc.vector.tensor_copy(out=b1f[:], in_=b1h[:])
        b2f = const.tile([P, NPAIR, 2], F32, name="b2f")
        nc.vector.tensor_copy(out=b2f[:], in_=b2h[:])

        xc = const.tile([P, NG * B], U32, name="xc", align_bytes=64)
        xs = const.tile([P, NG * B], U8, name="xs", align_bytes=64)
        hc = const.tile([P, NG * B], U32, name="hc", align_bytes=64)
        hs = const.tile([P, NG * B], U8, name="hs", align_bytes=64)
        sx_c = const.tile([P, B], F32, name="sx_c")
        sh_c = const.tile([P, B], F32, name="sh_c")

        tr_banks, grouped, codes, acc = {}, {}, {}, {}
        v1, h_bf, h_grp, v2, corrected = {}, {}, {}, {}, {}

        def t_step(q):
            for i in range(2):
                n = 2 * q + i
                src = w1_raw[n] if q < NPAIR else w2_val[n - 2 * NPAIR]
                for half in range(2):
                    tr_banks[q, i, half] = turn(src, 2 * half)

        def e_step(q):
            wg = grp.tile([P, 2, NG, P, 4], BF16, name="wg", align_bytes=64)
            grouped[q] = wg
            for i in range(2):
                for half in range(2):
                    bank = tr_banks.pop((q, i, half))
                    dst = wg[:, i, 2 * half : 2 * half + 2, :, :].bitcast(F32)
                    src = bank[:].rearrange("p g u r -> p g r u")
                    if 2 * i + half in E_VECTOR.get(q, ()):
                        nc.vector.tensor_copy(out=dst, in_=src)
                    else:
                        nc.scalar.copy(out=dst, in_=src)

        def q_step(q):
            wg = grouped.pop(q)
            wc = codep.tile([P, D // 2], U32, name="wc", align_bytes=64)
            ws = codep.tile([P, D // 2], U8, name="ws", align_bytes=64)
            nc.vector.quantize_mx(
                out=wc[:].bitcast(FP8X4), scales=ws[:], in_=wg[:].rearrange("p i g r t -> p (i g r t)")
            )
            codes[q] = (wc, ws)

        def m_step(q, passes):
            mc, ms = (xc, xs) if q < NPAIR else (hc, hs)
            for i in range(2):
                if passes[0] == 0:
                    bank = mmp.tile([P, B], F32, name="mm")
                    acc[q, i] = bank
                wc, ws = codes[q]
                for g in passes:
                    cols = slice((NG * i + g) * P, (NG * i + g + 1) * P)
                    nc.tensor.matmul_mx(
                        out=acc[q, i][:],
                        lhsT=wc[:, cols].bitcast(FP8X4),
                        lhsT_scale=ws[:, cols],
                        rhs=mc[:, g * B : (g + 1) * B].bitcast(FP8X4),
                        rhs_scale=ms[:, g * B : (g + 1) * B],
                        start=(g == 0),
                        stop=(g == NG - 1),
                    )

        def r_step(q):
            if q < NPAIR:
                grp_i = q // 2
                if q % 2 == 0:
                    v1_t = v1p.tile([P, 4, B], F32, name="v1_t")
                    v1[grp_i] = v1_t
                for i in range(2):
                    t = 2 * (q % 2) + i
                    nc.scalar.activation(
                        out=v1[grp_i][:, t, :], in_=acc.pop((q, i))[:], func=ACT.Relu,
                        bias=b1f[:, grp_i, t : t + 1], accum_out=m1pad[:, t, grp_i : grp_i + 1],
                    )
            else:
                j = q - NPAIR
                v2_t = rawp.tile([P, 2, B], F32, name="v2_t", tag="raw", align_bytes=64)
                v2[j] = v2_t
                for t in range(2):
                    nc.scalar.activation(
                        out=v2_t[:, t, :], in_=acc.pop((q, t))[:], func=ACT.Relu,
                        bias=b2f[:, j, t : t + 1], accum_out=m2pad[:, t, j : j + 1],
                    )

        def h_step(q):
            grp_i = q // 2
            if q % 2 == 0:
                h_t = hp.tile([P, 4, B], BF16, name="h_t", align_bytes=64)
                h_bf[grp_i] = h_t
            for i in range(2):
                t = 2 * (q % 2) + i
                nc.vector.scalar_tensor_tensor(
                    out=h_bf[grp_i][:, t, :], in0=sx_c[:], scalar=m1pad[:, t, grp_i : grp_i + 1],
                    in1=v1[grp_i][:, t, :], op0=ALU.mult, op1=ALU.add,
                )

        def h_group(g, engine_copy):
            hg = hp.tile([P, B, 4], BF16, name="hg", bufs=1, align_bytes=64)
            h_grp[g] = hg
            engine_copy(out=hg[:], in_=h_bf.pop(g)[:].rearrange("p t r -> p r t"))

        def h_quant(g):
            nc.vector.quantize_mx(
                out=hc[:, g * B : (g + 1) * B].bitcast(FP8X4), scales=hs[:, g * B : (g + 1) * B],
                in_=h_grp.pop(g)[:].rearrange("p r t -> p (r t)"),
            )

        def row_sums():
            bank = trp.tile([P, NRT, P], F32, name="tr")
            for rt in range(NRT):
                for n in range(16):
                    nc.tensor.matmul(
                        bank[:, rt, :], lhsT=v1[n // 4][:, n % 4, rt * P : (rt + 1) * P], rhs=ident[:],
                        start=(n == 0), stop=(n == 15), is_transpose=True,
                    )
            m1_sum = const.tile([P, 1], F32, name="m1_sum")
            nc.vector.tensor_reduce(out=m1_sum[:], in_=m1pad[:, :, 0:4], axis=AX.XY, op=ALU.add)
            tot = const.tile([P, NRT], F32, name="tot")
            nc.vector.tensor_reduce(out=tot[:], in_=bank[:], axis=AX.X, op=ALU.add)
            return m1_sum, tot

        def correct(j):
            o_t = rawp.tile([P, 2, B], F32, name="o_t", tag="raw", align_bytes=64)
            corrected[j] = o_t
            v2_t = v2.pop(j)
            for t in range(2):
                nc.vector.scalar_tensor_tensor(
                    out=o_t[:, t, :], in0=sh_c[:], scalar=m2pad[:, t, j : j + 1],
                    in1=v2_t[:, t, :], op0=ALU.mult, op1=ALU.add,
                )

        out_banks = {}

        def out_turn(j):
            o_t = corrected.pop(j)
            for b in range(2):
                bank = mmp.tile([P, 2, 2, P], F32, name="mm")
                out_banks[j, b] = bank
                for a in range(2):
                    rt = 2 * b + a
                    for t in range(2):
                        nc.tensor.transpose(bank[:, a, t, :], o_t[:, t, rt * P : (rt + 1) * P], ident[:])

        def out_store(j, both):
            o_sb = rawp.tile([P, NRT, P, 2], F32, name="o_sb", tag="raw", align_bytes=64)
            for b in range(2):
                bank = out_banks.pop((j, b))
                src = bank[:].rearrange("r a t p -> r a p t")
                if both and b == 1:
                    nc.vector.tensor_copy(out=o_sb[:, 2 * b : 2 * b + 2], in_=src)
                else:
                    nc.scalar.copy(out=o_sb[:, 2 * b : 2 * b + 2], in_=src)
                nc.sync.dma_start(
                    out=out_0.rearrange("(a r) (j c) -> j r a c", r=P, c=256)[j][:, 2 * b : 2 * b + 2, :],
                    in_=o_sb[:, 2 * b : 2 * b + 2].rearrange("r a p t -> r a (p t)"),
                )

        def means_out(pad, nt, rows, dst, name):
            bank = trp.tile([P, 4, P], F32, name="tr")
            for t in range(nt):
                nc.tensor.transpose(bank[:, t, :], pad[:, t, :], ident[:])
            m_sb = const.tile([P, P, nt], F32, name=name)
            nc.scalar.activation(
                out=m_sb[0:rows], in_=bank[0:rows, 0:nt, :].rearrange("g t p -> g p t"), func=ACT.Copy, scale=1.0 / B
            )
            nc.sync.dma_start(out=dst.rearrange("(g c) -> g c", g=rows), in_=m_sb[0:rows].rearrange("g p t -> g (p t)"))

        for q in range(2 * NPAIR + 2):
            if q >= 2:
                r_step(q - 2)

            if q == 17:
                out_turn(5)
                out_turn(6)
            elif q >= 12:
                out_turn(q - 12)
            if q < 2 * NPAIR:
                t_step(q)
                load_ahead(2 * q + 2)
            while len(w2_raw) < min(NPAIR, 3 + q, prod_next[0] // 2 + 4):
                load_w2(len(w2_raw))

            if q == 0:
                for g in range(NG):
                    nc.vector.quantize_mx(
                        out=xc[:, g * B : (g + 1) * B].bitcast(FP8X4), scales=xs[:, g * B : (g + 1) * B],
                        in_=xg[:, g].rearrange("p a r t -> p (a r t)"),
                    )
            if q == 2:
                sx_bank = mmp.tile([P, NRT, P], F32, name="mm")
                for rt in range(NRT):
                    nc.tensor.transpose(sx_bank[:, rt, :], sx_col[:, rt : rt + 1].to_broadcast([P, P]), ident[:])
                nc.scalar.activation(
                    out=sx_c[:], in_=sx_bank[:].rearrange("p a r -> p (a r)"), func=ACT.Copy, scale=COEF / B
                )

            if 0 <= q - 2 < NPAIR:
                h_step(q - 2)
            if q == 16:
                correct(5)
                correct(6)
            elif q == 17:
                correct(7)
            elif q >= 11:
                correct(q - 11)

            if q < 2 * NPAIR:
                e_step(q)
            for rt in SUMS.get(q + 1, ()):
                x_sum(rt)
            if q < NPAIR:
                load_ahead(2 * q + 2)
            if q in (3, 5, 7):
                h_group((q - 3) // 2, nc.scalar.copy)
            if q == 9:
                h_group(3, nc.vector.tensor_copy)
            if q < 2 * NPAIR:
                products(PROD[q])
            if q == 9:
                h_quant(3)
            if q < 2 * NPAIR:
                q_step(q)
            if q in (4, 6, 8):
                h_quant((q - 4) // 2)

            if q == 17:
                out_store(5, True)
                out_store(6, True)
            elif q >= 12:
                out_store(q - 12, False)

            if q == 9:
                m_step(8, (0, 1, 2))
                m1_sum, tot = row_sums()
                m_step(8, (3,))
            elif 1 <= q <= 2 * NPAIR:
                m_step(q - 1, (0, 1, 2, 3))
            if q == 10:
                bank = trp.tile([P, 1], F32, name="tr")
                nc.tensor.matmul(bank[:], lhsT=ones_f[:], rhs=m1_sum[:], start=True, stop=True)
                m1_tot = const.tile([P, 1], F32, name="m1_tot")
                nc.vector.tensor_copy(out=m1_tot[:], in_=bank[:])
                sh_h = const.tile([P, B], F32, name="sh_h")
                bank2 = trp.tile([P, NRT, P], F32, name="tr")
                for rt in range(NRT):
                    nc.tensor.transpose(bank2[:, rt, :], tot[:, rt : rt + 1].to_broadcast([P, P]), ident[:])
                nc.vector.scalar_tensor_tensor(
                    out=sh_h[:], in0=sx_c[:], scalar=m1_tot[:], in1=bank2[:].rearrange("p a r -> p (a r)"),
                    op0=ALU.mult, op1=ALU.add,
                )
                nc.scalar.activation(out=sh_c[:], in_=sh_h[:], func=ACT.Copy, scale=COEF / B)
                means_out(m1pad, 4, 4, out_1, "m1_sb")

        means_out(m2pad, 2, 8, out_2, "m2_sb")
        out_turn(7)
        out_store(7, True)
